import numpy as np
import ml_dtypes


def mxq(x, axis, fmt="e4m3"):
    dtype, down = {"e4m3": (ml_dtypes.float8_e4m3fn, 7), "e5m2": (ml_dtypes.float8_e5m2, 14)}[fmt]
    v = np.moveaxis(np.asarray(x, np.float32).astype(ml_dtypes.bfloat16).astype(np.float64), axis, -1)
    blocks = v.reshape(v.shape[:-1] + (-1, 32))
    amax = np.abs(blocks).max(-1, keepdims=True)
    byte = np.maximum(np.where(amax > 0, np.frexp(amax)[1] - 1 + 127, 0) - down, 1)
    scale = np.exp2(byte - 127.0)
    codes = (blocks / scale).astype(np.float32).astype(dtype).astype(np.float64)
    return np.moveaxis((codes * scale).reshape(v.shape), -1, axis)


WIDE = False


def mx_kscale(k):
    if not WIDE:
        return np.ones(k)
    levels = np.array([10, -10, 5, -5, 0])
    if k % 512:
        return np.exp2(np.random.permutation(np.resize(levels, k // 32))).repeat(32)
    a = np.empty((k // 512, 16))
    for p in range(k // 512):
        a[p, :8] = np.random.permutation(np.resize(levels, 8))
        for g in range(8):
            far = levels[np.abs(levels - a[p, g]) >= 10]
            a[p, g + 8] = far[np.random.randint(len(far))]
    return np.exp2(a.ravel()).repeat(32)


BF16 = ml_dtypes.bfloat16


def bf(x):
    return np.asarray(x, np.float32).astype(BF16)


def f64(x):
    return np.asarray(x).astype(np.float64)


B, N, F, D, DIM = 2, 512, 512, 2048, 32
EPS = 1e-6
RAD = 3.0


def expmap0_full(us):
    r = np.sqrt((us * us).sum(-1, keepdims=True))
    rs = np.maximum(r, EPS)
    x0 = 0.5 * (np.exp(r) + np.exp(-r))
    xs = (0.5 * (np.exp(rs) - np.exp(-rs)) / rs) * us
    return np.concatenate([x0, xs], axis=-1)


def draw0():
    s = mx_kscale(F)
    amp = 0.5 + 0.5 * np.random.random((B, N, 1))
    return {"x": bf(np.random.standard_normal((B, N, F)) * amp * s),
            "w_sp": bf(np.random.standard_normal((F, D)) * RAD / np.sqrt(D * F) / s[:, None])}


def core(x, w_sp):
    us = mxq(f64(x), 2, "e4m3") @ mxq(f64(w_sp), 0, "e4m3")
    return expmap0_full(us)


def e4m3fn_bytes(y):
    return np.clip(np.asarray(y, np.float64), -448.0, 448.0).astype(np.float32).astype(ml_dtypes.float8_e4m3fn).view(np.uint8)


def e4m3fn_values(b):
    return np.asarray(b, np.uint8).view(ml_dtypes.float8_e4m3fn).astype(np.float64)


def setup_inputs():
    d = draw0()
    x0 = np.asarray(d['w_sp']).astype(np.float64)
    s = (np.max(np.abs(x0), axis=(1,), keepdims=True) / 448.0).astype(np.float32)
    out = {}
    for k, v in d.items():
        if k == 'w_sp':
            out['w_sp_bytes'] = e4m3fn_bytes(x0 / s.astype(np.float64))
            out['w_sp_scale'] = s
        else:
            out[k] = v
    return out


def reference(x, w_sp_bytes, w_sp_scale):
    return core(x, e4m3fn_values(w_sp_bytes) * w_sp_scale.astype(np.float64))

@@ -1,0 +1,291 @@
+from contextlib import ExitStack
+import math
+
+import concourse.mybir as mybir
+from concourse.masks import make_identity
+
+F32 = mybir.dt.float32
+BF16 = mybir.dt.bfloat16
+U8 = mybir.dt.uint8
+U32 = mybir.dt.uint32
+FP8 = mybir.dt.float8_e4m3fn
+FP8X4 = mybir.dt.float8_e4m3fn_x4
+ACT = mybir.ActivationFunctionType
+ALU = mybir.AluOpType
+
+P = 128
+K = 512
+D = 2048
+TILES = 8
+BANK = 512
+ROW = D + 1
+EPS = 1e-6
+FLOPS = 2 * 1024 * K * D
+
+V_PIECES = ((0, 512), (512, 1024), (1024, 1280))
+S_PIECES = ((1536, 2048), (1280, 1536))
+
+
+def tile_hgcn_pb_kernel(tc, x, w_sp_bytes, w_sp_scale, out):
+    nc = tc.nc
+    x_v = x.rearrange("b (q j) k -> (b q) j k", j=TILES)
+    w_v = w_sp_bytes.rearrange("(p t) n -> p t n", t=4)
+    s_v = w_sp_scale.rearrange("(p t) o -> p (t o)", t=4)
+    out_v = out.rearrange("b (q j) c -> (b q) (j c)", j=TILES)
+
+    with ExitStack() as ctx:
+        keep = ctx.enter_context(tc.tile_pool(name="keep", bufs=1))
+        scrap = ctx.enter_context(tc.tile_pool(name="scrap", bufs=2))
+        psum = ctx.enter_context(tc.psum_pool(name="psum", bufs=8))
+
+        ident = keep.tile([P, P], F32, name="ident")
+        w_scale = keep.tile([P, 4], F32, name="w_scale")
+        plus_minus = keep.tile([P, 2], F32, name="plus_minus")
+        half = keep.tile([P, 1], F32, name="half")
+        warm = keep.tile([P, 1], F32, name="warm")
+        w_bytes = []
+        w_wide = []
+        for c in range(4):
+            w_bytes.append(keep.tile([P, 4, BANK], U8, name="w_bytes%d" % c))
+            w_wide.append(keep.tile([P, 4, BANK], BF16, name="w_wide%d" % c))
+        w_group = keep.tile([P, 4 * D], BF16, name="w_group", align_bytes=64)
+        w_codes = keep.tile([P, D], U32, name="w_codes", align_bytes=64)
+        w_scales = keep.tile([P, D], U8, name="w_scales", align_bytes=64)
+        x_sb = keep.tile([P, TILES, K], BF16, name="x_sb")
+        x_group = keep.tile([P, TILES * K], BF16, name="x_group", align_bytes=64)
+        x_codes = keep.tile([P, TILES * P], U32, name="x_codes", align_bytes=64)
+        x_scales = keep.tile([P, TILES * P], U8, name="x_scales", align_bytes=64)
+        result = keep.tile([P, TILES * ROW], F32, name="result")
+        sumsq = keep.tile([P, 4 * TILES], F32, name="sumsq")
+        part = keep.tile([P, TILES], F32, name="part")
+        normsq = keep.tile([P, TILES], F32, name="normsq")
+        radius = keep.tile([P, TILES], F32, name="radius")
+        inv_radius = keep.tile([P, TILES], F32, name="inv_radius")
+        halves = keep.tile([P, 2 * TILES], F32, name="halves")
+        factor = keep.tile([P, TILES], F32, name="factor")
+
+        x_words = x_sb[:].rearrange("p j k -> p (j k)").bitcast(F32)
+        xg_words = x_group[:].bitcast(F32)
+
+        nc.scalar.dma_start(out=w_scale[:], in_=s_v)
+
+        def load_w(c):
+            nc.sync.dma_start(out=w_bytes[c][:], in_=w_v[:, :, c * BANK:(c + 1) * BANK])
+
+        load_w(0)
+        load_w(3)
+        nc.sync.dma_start(out=x_sb[:, 0:2, :], in_=x_v[:, 0:2, :])
+        load_w(1)
+        load_w(2)
+        nc.sync.dma_start(out=x_sb[:, 2:TILES, :], in_=x_v[:, 2:TILES, :])
+
+        nc.vector.memset(half[:], 0.5)
+        nc.vector.memset(plus_minus[:, 0:1], 1.0)
+        nc.vector.memset(plus_minus[:, 1:2], -1.0)
+        nc.scalar.activation(out=warm[:], in_=half[:], func=ACT.Exp)
+        make_identity(nc, ident[:])
+
+        def widen(on_scalar, piece):
+            c = piece[0] // BANK
+            a = piece[0] - c * BANK
+            b = piece[1] - c * BANK
+            for t in range(4):
+                src = w_bytes[c][:, t, a:b].bitcast(FP8)
+                dst = w_wide[c][:, t, a:b]
+                if on_scalar:
+                    nc.scalar.activation(out=dst, in_=src, func=ACT.Copy, scale=w_scale[:, t:t + 1])
+                else:
+                    nc.vector.tensor_scalar(out=dst, in0=src, scalar1=w_scale[:, t:t + 1], scalar2=None, op0=ALU.mult)
+
+        def interleave(on_scalar, piece):
+            c = piece[0] // BANK
+            a = piece[0] - c * BANK
+            b = piece[1] - c * BANK
+            src = w_wide[c][:, :, a:b].rearrange("p t n -> p n t")
+            dst = w_group[:, 4 * piece[0]:4 * piece[1]].rearrange("p (n t) -> p n t", t=4)
+            if on_scalar:
+                nc.scalar.copy(out=dst, in_=src)
+            else:
+                nc.vector.tensor_copy(out=dst, in_=src)
+
+        def quantize_w(piece):
+            n0, n1 = piece
+            nc.vector.quantize_mx(
+                out=w_codes[:, n0:n1].bitcast(FP8X4),
+                scales=w_scales[:, n0:n1],
+                in_=w_group[:, 4 * n0:4 * n1],
+            )
+
+        def transpose_pair(g):
+            xt = psum.tile([P, BANK], F32, name="xt", tag="bank")
+            for jj in range(2):
+                for u in range(2):
+                    j = 2 * g + jj
+                    s = 2 * jj + u
+                    nc.tensor.transpose(
+                        xt[:, s * P:(s + 1) * P],
+                        x_words[:, 256 * j + u:256 * (j + 1):2],
+                        ident[:],
+                    )
+            return xt
+
+        def copy_pair(on_scalar, g, xt):
+            dst = xg_words[:, BANK * g:BANK * (g + 1)].rearrange("p (j r u) -> p j r u", j=2, u=2)
+            src = xt[:].rearrange("p (j u r) -> p j r u", j=2, u=2)
+            if on_scalar:
+                nc.scalar.copy(out=dst, in_=src)
+            else:
+                nc.vector.tensor_copy(out=dst, in_=src)
+
+        def quantize_x(g):
+            nc.vector.quantize_mx(
+                out=x_codes[:, 256 * g:256 * (g + 1)].bitcast(FP8X4),
+                scales=x_scales[:, 256 * g:256 * (g + 1)],
+                in_=x_group[:, 1024 * g:1024 * (g + 1)],
+            )
+
+        acc = {}
+
+        def product(i, c):
+            bank = psum.tile([P, BANK], F32, name="acc", tag="bank")
+            nc.tensor.matmul_mx(
+                out=bank[:],
+                lhsT=x_codes[:, P * i:P * (i + 1)].bitcast(FP8X4),
+                lhsT_scale=x_scales[:, P * i:P * (i + 1)],
+                rhs=w_codes[:, BANK * c:BANK * (c + 1)].bitcast(FP8X4),
+                rhs_scale=w_scales[:, BANK * c:BANK * (c + 1)],
+                start=True,
+                stop=True,
+            )
+            acc[(i, c)] = bank
+
+        def square_sum(i, c, pos):
+            junk = scrap.tile([P, BANK], BF16, name="junk")
+            nc.scalar.activation(
+                out=junk[:], in_=acc[(i, c)][:], func=ACT.Square,
+                accum_out=sumsq[:, 4 * i + pos:4 * i + pos + 1],
+            )
+
+        def norm(i):
+            s = 4 * i
+            nc.gpsimd.tensor_scalar(
+                out=part[:, i:i + 1], in0=sumsq[:, s:s + 1],
+                scalar1=sumsq[:, s + 1:s + 2], scalar2=sumsq[:, s + 2:s + 3],
+                op0=ALU.add, op1=ALU.add,
+            )
+            nc.gpsimd.tensor_scalar(
+                out=normsq[:, i:i + 1], in0=sumsq[:, s + 3:s + 4],
+                scalar1=part[:, i:i + 1], scalar2=EPS * EPS,
+                op0=ALU.add, op1=ALU.max,
+            )
+            nc.gpsimd.tensor_tensor(out=radius[:, i:i + 1], in0=normsq[:, i:i + 1], in1=half[:], op=ALU.pow)
+
+        def exponentials(i):
+            nc.scalar.activation(
+                out=halves[:, 2 * i:2 * i + 2], in_=plus_minus[:], func=ACT.Exp,
+                scale=radius[:, i:i + 1], bias=-math.log(2.0),
+                accum_out=result[:, ROW * i:ROW * i + 1],
+            )
+
+        def make_factor(i):
+            nc.vector.reciprocal(out=inv_radius[:, i:i + 1], in_=radius[:, i:i + 1])
+            nc.vector.tensor_scalar(
+                out=factor[:, i:i + 1], in0=halves[:, 2 * i:2 * i + 1],
+                scalar1=halves[:, 2 * i + 1:2 * i + 2], scalar2=inv_radius[:, i:i + 1],
+                op0=ALU.subtract, op1=ALU.mult,
+            )
+
+        def scale_out(on_scalar, i, c):
+            lo = ROW * i + 1 + BANK * c
+            dst = result[:, lo:lo + BANK]
+            if on_scalar:
+                nc.scalar.activation(out=dst, in_=acc[(i, c)][:], func=ACT.Copy, scale=factor[:, i:i + 1])
+            else:
+                nc.vector.tensor_scalar(out=dst, in0=acc[(i, c)][:], scalar1=factor[:, i:i + 1], scalar2=None, op0=ALU.mult)
+
+        def store(lo, hi):
+            nc.sync.dma_start(out=out_v[:, lo:hi], in_=result[:, lo:hi])
+
+        ctx.enter_context(tc.manual_schedule())
+        xt_a = transpose_pair(0)
+        widen(False, V_PIECES[0])
+        widen(True, S_PIECES[0])
+        copy_pair(True, 0, xt_a)
+        interleave(False, V_PIECES[0])
+        widen(False, V_PIECES[1])
+        quantize_w(V_PIECES[0])
+        quantize_x(0)
+        interleave(True, S_PIECES[0])
+        product(0, 0)
+        product(1, 0)
+        interleave(False, V_PIECES[1])
+        widen(False, V_PIECES[2])
+        quantize_w(V_PIECES[1])
+        product(0, 1)
+        product(1, 1)
+        xt_b = transpose_pair(1)
+        xt_c = transpose_pair(2)
+        widen(True, S_PIECES[1])
+        interleave(True, S_PIECES[1])
+        interleave(False, V_PIECES[2])
+        quantize_w(S_PIECES[0])
+        product(0, 3)
+        quantize_w(V_PIECES[2])
+        quantize_w(S_PIECES[1])
+        product(0, 2)
+        square_sum(0, 0, 0)
+        square_sum(0, 1, 1)
+        square_sum(0, 3, 2)
+        square_sum(0, 2, 3)
+        norm(0)
+        copy_pair(False, 1, xt_b)
+        copy_pair(False, 2, xt_c)
+        square_sum(1, 0, 0)
+        square_sum(1, 1, 1)
+        exponentials(0)
+        xt_d = transpose_pair(3)
+        product(1, 2)
+        quantize_x(1)
+        copy_pair(False, 3, xt_d)
+        product(1, 3)
+        make_factor(0)
+        square_sum(1, 2, 2)
+        square_sum(1, 3, 3)
+        norm(1)
+        for c in range(4):
+            scale_out(False, 0, c)
+            product(2, c)
+            if c == 1:
+                store(0, 1024)
+        store(1024, 2048)
+        quantize_x(2)
+
+        last = TILES - 1
+        for i in range(2, TILES):
+            square_sum(i, 0, 0)
+            square_sum(i, 1, 1)
+            exponentials(i - 1)
+            make_factor(i - 1)
+            square_sum(i, 2, 2)
+            square_sum(i, 3, 3)
+            norm(i)
+            for c in range(4):
+                scale_out(i == last and c >= 2, i - 1, c)
+                if i < last:
+                    product(i + 1, c)
+                if i == last and c == 1:
+                    store(D * (i - 1), D * (i - 1) + 1024)
+            if i == last:
+                store(D * (i - 1) + 1024, D * i)
+            else:
+                store(D * (i - 1), D * i)
+            if i == 2:
+                quantize_x(3)
+
+        exponentials(last)
+        make_factor(last)
+        for c in range(4):
+            scale_out(c % 2 == 1, last, c)
+            if c == 1:
+                store(D * last, D * last + 1024)
+        store(D * last + 1024, TILES * ROW)

@@ -22,8 +22,17 @@ ROW = D + 1
 EPS = 1e-6
 FLOPS = 2 * 1024 * K * D
 
-V_PIECES = ((0, 512), (512, 1024), (1024, 1280))
-S_PIECES = ((1536, 2048), (1280, 1536))
+W0 = (0, 512)
+W1 = (512, 1024)
+W2 = (1024, 1536)
+W3 = (1536, 2048)
+N_STEPS = 4 * TILES
+B_START = 8
+EXP_FIRST = 2
+EXP_AFTER = 3
+FAC_DELAY = 2
+S_HELP = (25, 27, 29, 31)
+LAST_EXP = 25
 
 
 def tile_hgcn_pb_kernel(tc, x, w_sp_bytes, w_sp_scale, out):
@@ -36,7 +45,7 @@ def tile_hgcn_pb_kernel(tc, x, w_sp_bytes, w_sp_scale, out):
     with ExitStack() as ctx:
         keep = ctx.enter_context(tc.tile_pool(name="keep", bufs=1))
         scrap = ctx.enter_context(tc.tile_pool(name="scrap", bufs=2))
-        psum = ctx.enter_context(tc.psum_pool(name="psum", bufs=8))
+        psum = ctx.enter_context(tc.psum_pool(name="psum", bufs=4))
 
         ident = keep.tile([P, P], F32, name="ident")
         w_scale = keep.tile([P, 4], F32, name="w_scale")
@@ -72,12 +81,14 @@ def tile_hgcn_pb_kernel(tc, x, w_sp_bytes, w_sp_scale, out):
         def load_w(c):
             nc.sync.dma_start(out=w_bytes[c][:], in_=w_v[:, :, c * BANK:(c + 1) * BANK])
 
-        load_w(0)
-        load_w(3)
+        for t in range(4):
+            for c in (0, 3):
+                nc.sync.dma_start(out=w_bytes[c][:, t, :], in_=w_v[:, t, c * BANK:(c + 1) * BANK])
         nc.sync.dma_start(out=x_sb[:, 0:2, :], in_=x_v[:, 0:2, :])
         load_w(1)
+        nc.sync.dma_start(out=x_sb[:, 2:4, :], in_=x_v[:, 2:4, :])
         load_w(2)
-        nc.sync.dma_start(out=x_sb[:, 2:TILES, :], in_=x_v[:, 2:TILES, :])
+        nc.sync.dma_start(out=x_sb[:, 4:TILES, :], in_=x_v[:, 4:TILES, :])
 
         nc.vector.memset(half[:], 0.5)
         nc.vector.memset(plus_minus[:, 0:1], 1.0)
@@ -117,7 +128,7 @@ def tile_hgcn_pb_kernel(tc, x, w_sp_bytes, w_sp_scale, out):
             )
 
         def transpose_pair(g):
-            xt = psum.tile([P, BANK], F32, name="xt", tag="bank")
+            xt = psum.tile([P, BANK], F32, name="xt", tag="out")
             for jj in range(2):
                 for u in range(2):
                     j = 2 * g + jj
@@ -146,8 +157,8 @@ def tile_hgcn_pb_kernel(tc, x, w_sp_bytes, w_sp_scale, out):
 
         acc = {}
 
-        def product(i, c):
-            bank = psum.tile([P, BANK], F32, name="acc", tag="bank")
+        def product(i, c, stream):
+            bank = psum.tile([P, BANK], F32, name="acc_" + stream, tag=stream)
             nc.tensor.matmul_mx(
                 out=bank[:],
                 lhsT=x_codes[:, P * i:P * (i + 1)].bitcast(FP8X4),
@@ -157,12 +168,12 @@ def tile_hgcn_pb_kernel(tc, x, w_sp_bytes, w_sp_scale, out):
                 start=True,
                 stop=True,
             )
-            acc[(i, c)] = bank
+            acc[(stream, i, c)] = bank
 
         def square_sum(i, c, pos):
             junk = scrap.tile([P, BANK], BF16, name="junk")
             nc.scalar.activation(
-                out=junk[:], in_=acc[(i, c)][:], func=ACT.Square,
+                out=junk[:], in_=acc[("sq", i, c)][:], func=ACT.Square,
                 accum_out=sumsq[:, 4 * i + pos:4 * i + pos + 1],
             )
 
@@ -199,93 +210,90 @@ def tile_hgcn_pb_kernel(tc, x, w_sp_bytes, w_sp_scale, out):
             lo = ROW * i + 1 + BANK * c
             dst = result[:, lo:lo + BANK]
             if on_scalar:
-                nc.scalar.activation(out=dst, in_=acc[(i, c)][:], func=ACT.Copy, scale=factor[:, i:i + 1])
+                nc.scalar.activation(out=dst, in_=acc[("out", i, c)][:], func=ACT.Copy, scale=factor[:, i:i + 1])
             else:
-                nc.vector.tensor_scalar(out=dst, in0=acc[(i, c)][:], scalar1=factor[:, i:i + 1], scalar2=None, op0=ALU.mult)
+                nc.vector.tensor_scalar(out=dst, in0=acc[("out", i, c)][:], scalar1=factor[:, i:i + 1], scalar2=None, op0=ALU.mult)
 
         def store(lo, hi):
             nc.sync.dma_start(out=out_v[:, lo:hi], in_=result[:, lo:hi])
 
-        ctx.enter_context(tc.manual_schedule())
-        xt_a = transpose_pair(0)
-        widen(False, V_PIECES[0])
-        widen(True, S_PIECES[0])
-        copy_pair(True, 0, xt_a)
-        interleave(False, V_PIECES[0])
-        widen(False, V_PIECES[1])
-        quantize_w(V_PIECES[0])
-        quantize_x(0)
-        interleave(True, S_PIECES[0])
-        product(0, 0)
-        product(1, 0)
-        interleave(False, V_PIECES[1])
-        widen(False, V_PIECES[2])
-        quantize_w(V_PIECES[1])
-        product(0, 1)
-        product(1, 1)
-        xt_b = transpose_pair(1)
-        xt_c = transpose_pair(2)
-        widen(True, S_PIECES[1])
-        interleave(True, S_PIECES[1])
-        interleave(False, V_PIECES[2])
-        quantize_w(S_PIECES[0])
-        product(0, 3)
-        quantize_w(V_PIECES[2])
-        quantize_w(S_PIECES[1])
-        product(0, 2)
-        square_sum(0, 0, 0)
-        square_sum(0, 1, 1)
-        square_sum(0, 3, 2)
-        square_sum(0, 2, 3)
-        norm(0)
-        copy_pair(False, 1, xt_b)
-        copy_pair(False, 2, xt_c)
-        square_sum(1, 0, 0)
-        square_sum(1, 1, 1)
-        exponentials(0)
-        xt_d = transpose_pair(3)
-        product(1, 2)
-        quantize_x(1)
-        copy_pair(False, 3, xt_d)
-        product(1, 3)
-        make_factor(0)
-        square_sum(1, 2, 2)
-        square_sum(1, 3, 3)
-        norm(1)
-        for c in range(4):
-            scale_out(False, 0, c)
-            product(2, c)
-            if c == 1:
-                store(0, 1024)
-        store(1024, 2048)
-        quantize_x(2)
-
-        last = TILES - 1
-        for i in range(2, TILES):
-            square_sum(i, 0, 0)
-            square_sum(i, 1, 1)
-            exponentials(i - 1)
-            make_factor(i - 1)
-            square_sum(i, 2, 2)
-            square_sum(i, 3, 3)
-            norm(i)
+        a_order = [(0, 0), (1, 0), (0, 1), (1, 1), (2, 0), (0, 3), (0, 2), (1, 3), (1, 2), (2, 1), (2, 3), (2, 2)]
+        for i in range(3, TILES):
             for c in range(4):
-                scale_out(i == last and c >= 2, i - 1, c)
-                if i < last:
-                    product(i + 1, c)
-                if i == last and c == 1:
-                    store(D * (i - 1), D * (i - 1) + 1024)
-            if i == last:
-                store(D * (i - 1) + 1024, D * i)
-            else:
-                store(D * (i - 1), D * i)
-            if i == 2:
-                quantize_x(3)
+                a_order.append((i, c))
+        seen = {}
+        pos_of = []
+        last_step = {}
+        for n in range(N_STEPS):
+            i = a_order[n][0]
+            pos_of.append(seen.get(i, 0))
+            seen[i] = seen.get(i, 0) + 1
+            last_step[i] = n
+        exp_at = {}
+        fac_at = {}
+        for i in range(TILES - 1):
+            k = last_step[i] + (EXP_FIRST if i == 0 else EXP_AFTER)
+            exp_at[k] = i
+            fac_at[k + (0 if i == 0 else FAC_DELAY)] = i
+        cuts = {0: [(0, 512)], 1: [(512, 1024)], 3: [(1024, 2048)]}
+        for i in range(1, TILES - 1):
+            for h in range(2):
+                cuts[4 * i + 1 + 2 * h] = [(D * i + 1024 * h, D * i + 1024 * (h + 1))]
+        for c in range(3):
+            cuts[4 * (TILES - 1) + c] = [(D * (TILES - 1) + BANK * c, D * (TILES - 1) + BANK * (c + 1))]
+        cuts[N_STEPS - 1] = [(D * (TILES - 1) + BANK * 3, TILES * ROW)]
 
-        exponentials(last)
-        make_factor(last)
-        for c in range(4):
-            scale_out(c % 2 == 1, last, c)
-            if c == 1:
-                store(D * last, D * last + 1024)
-        store(D * last + 1024, TILES * ROW)
+        ctx.enter_context(tc.manual_schedule())
+        xts = {}
+        xts[0] = transpose_pair(0)
+        widen(False, W0)
+        widen(True, W3)
+        copy_pair(True, 0, xts[0])
+        interleave(False, W0)
+        widen(False, W1)
+        quantize_w(W0)
+        quantize_x(0)
+        interleave(True, W3)
+        for g in (1, 2, 3):
+            xts[g] = transpose_pair(g)
+        copy_pair(True, 1, xts[1])
+        interleave(False, W1)
+        widen(False, W2)
+        quantize_w(W1)
+        quantize_x(1)
+        interleave(False, W2)
+        quantize_w(W3)
+        quantize_w(W2)
+        for n in range(4):
+            product(a_order[n][0], a_order[n][1], "sq")
+        m = 0
+        for n in range(N_STEPS + B_START + 1):
+            if n < N_STEPS:
+                i, c = a_order[n]
+                square_sum(i, c, pos_of[n])
+                if n + 4 < N_STEPS:
+                    product(a_order[n + 4][0], a_order[n + 4][1], "sq")
+            if n in exp_at:
+                exponentials(exp_at[n])
+            if n in fac_at:
+                make_factor(fac_at[n])
+            if n < N_STEPS and last_step[a_order[n][0]] == n:
+                norm(a_order[n][0])
+            if n == 1:
+                copy_pair(True, 2, xts[2])
+                copy_pair(False, 3, xts[3])
+                quantize_x(2)
+                quantize_x(3)
+            if n == B_START:
+                for c in range(4):
+                    product(0, c, "out")
+            if n > B_START:
+                scale_out(m in S_HELP, m // 4, m % 4)
+                if m + 4 < N_STEPS:
+                    product((m + 4) // 4, (m + 4) % 4, "out")
+                for lo, hi in cuts.get(m, []):
+                    store(lo, hi)
+                if m == LAST_EXP:
+                    exponentials(TILES - 1)
+                    make_factor(TILES - 1)
+                m += 1

@@ -30,9 +30,9 @@ N_STEPS = 4 * TILES
 B_START = 8
 EXP_FIRST = 2
 EXP_AFTER = 3
-FAC_DELAY = 2
+FAC_DELAY = 0
 S_HELP = (25, 27, 29, 31)
-LAST_EXP = 25
+LAST_EXP = 27
 
 
 def tile_hgcn_pb_kernel(tc, x, w_sp_bytes, w_sp_scale, out):
@@ -51,6 +51,7 @@ def tile_hgcn_pb_kernel(tc, x, w_sp_bytes, w_sp_scale, out):
         w_scale = keep.tile([P, 4], F32, name="w_scale")
         plus_minus = keep.tile([P, 2], F32, name="plus_minus")
         half = keep.tile([P, 1], F32, name="half")
+        minus_half = keep.tile([P, 1], F32, name="minus_half")
         warm = keep.tile([P, 1], F32, name="warm")
         w_bytes = []
         w_wide = []
@@ -72,6 +73,8 @@ def tile_hgcn_pb_kernel(tc, x, w_sp_bytes, w_sp_scale, out):
         inv_radius = keep.tile([P, TILES], F32, name="inv_radius")
         halves = keep.tile([P, 2 * TILES], F32, name="halves")
         factor = keep.tile([P, TILES], F32, name="factor")
+        inv_radius_first = keep.tile([P, 1], F32, name="inv_radius_first")
+        factor_first = keep.tile([P, 1], F32, name="factor_first")
 
         x_words = x_sb[:].rearrange("p j k -> p (j k)").bitcast(F32)
         xg_words = x_group[:].bitcast(F32)
@@ -91,6 +94,7 @@ def tile_hgcn_pb_kernel(tc, x, w_sp_bytes, w_sp_scale, out):
         nc.sync.dma_start(out=x_sb[:, 4:TILES, :], in_=x_v[:, 4:TILES, :])
 
         nc.vector.memset(half[:], 0.5)
+        nc.vector.memset(minus_half[:], -0.5)
         nc.vector.memset(plus_minus[:, 0:1], 1.0)
         nc.vector.memset(plus_minus[:, 1:2], -1.0)
         nc.scalar.activation(out=warm[:], in_=half[:], func=ACT.Exp)
@@ -190,6 +194,8 @@ def tile_hgcn_pb_kernel(tc, x, w_sp_bytes, w_sp_scale, out):
                 op0=ALU.add, op1=ALU.max,
             )
             nc.gpsimd.tensor_tensor(out=radius[:, i:i + 1], in0=normsq[:, i:i + 1], in1=half[:], op=ALU.pow)
+            if i > 0:
+                nc.gpsimd.tensor_tensor(out=inv_radius[:, i:i + 1], in0=normsq[:, i:i + 1], in1=minus_half[:], op=ALU.pow)
 
         def exponentials(i):
             nc.scalar.activation(
@@ -198,21 +204,31 @@ def tile_hgcn_pb_kernel(tc, x, w_sp_bytes, w_sp_scale, out):
                 accum_out=result[:, ROW * i:ROW * i + 1],
             )
 
+        def factor_of(i):
+            return factor_first[:] if i == 0 else factor[:, i:i + 1]
+
         def make_factor(i):
-            nc.vector.reciprocal(out=inv_radius[:, i:i + 1], in_=radius[:, i:i + 1])
-            nc.vector.tensor_scalar(
-                out=factor[:, i:i + 1], in0=halves[:, 2 * i:2 * i + 1],
-                scalar1=halves[:, 2 * i + 1:2 * i + 2], scalar2=inv_radius[:, i:i + 1],
-                op0=ALU.subtract, op1=ALU.mult,
-            )
+            if i == 0:
+                nc.vector.reciprocal(out=inv_radius_first[:], in_=radius[:, 0:1])
+                nc.vector.tensor_scalar(
+                    out=factor_first[:], in0=halves[:, 0:1],
+                    scalar1=halves[:, 1:2], scalar2=inv_radius_first[:],
+                    op0=ALU.subtract, op1=ALU.mult,
+                )
+            else:
+                nc.gpsimd.tensor_scalar(
+                    out=factor[:, i:i + 1], in0=halves[:, 2 * i:2 * i + 1],
+                    scalar1=halves[:, 2 * i + 1:2 * i + 2], scalar2=inv_radius[:, i:i + 1],
+                    op0=ALU.subtract, op1=ALU.mult,
+                )
 
         def scale_out(on_scalar, i, c):
             lo = ROW * i + 1 + BANK * c
             dst = result[:, lo:lo + BANK]
             if on_scalar:
-                nc.scalar.activation(out=dst, in_=acc[("out", i, c)][:], func=ACT.Copy, scale=factor[:, i:i + 1])
+                nc.scalar.activation(out=dst, in_=acc[("out", i, c)][:], func=ACT.Copy, scale=factor_of(i))
             else:
-                nc.vector.tensor_scalar(out=dst, in0=acc[("out", i, c)][:], scalar1=factor[:, i:i + 1], scalar2=None, op0=ALU.mult)
+                nc.vector.tensor_scalar(out=dst, in0=acc[("out", i, c)][:], scalar1=factor_of(i), scalar2=None, op0=ALU.mult)
 
         def store(lo, hi):
             nc.sync.dma_start(out=out_v[:, lo:hi], in_=result[:, lo:hi])
@@ -280,7 +296,7 @@ def tile_hgcn_pb_kernel(tc, x, w_sp_bytes, w_sp_scale, out):
             if n < N_STEPS and last_step[a_order[n][0]] == n:
                 norm(a_order[n][0])
             if n == 1:
-                copy_pair(True, 2, xts[2])
+                copy_pair(False, 2, xts[2])
                 copy_pair(False, 3, xts[3])
                 quantize_x(2)
                 quantize_x(3)

@@ -116,8 +116,8 @@ def tile_hgcn_pb_kernel(tc, x, w_sp_bytes, w_sp_scale, out):
             c = piece[0] // BANK
             a = piece[0] - c * BANK
             b = piece[1] - c * BANK
-            src = w_wide[c][:, :, a:b].rearrange("p t n -> p n t")
-            dst = w_group[:, 4 * piece[0]:4 * piece[1]].rearrange("p (n t) -> p n t", t=4)
+            src = w_wide[c][:, :, a:b].rearrange("p t (g i) -> p g t i", i=4)
+            dst = w_group[:, 4 * piece[0]:4 * piece[1]].rearrange("p (g i t) -> p g t i", i=4, t=4)
             if on_scalar:
                 nc.scalar.copy(out=dst, in_=src)
             else:

@@ -84,9 +84,14 @@ def tile_hgcn_pb_kernel(tc, x, w_sp_bytes, w_sp_scale, out):
         def load_w(c):
             nc.sync.dma_start(out=w_bytes[c][:], in_=w_v[:, :, c * BANK:(c + 1) * BANK])
 
-        for t in range(4):
-            for c in (0, 3):
-                nc.sync.dma_start(out=w_bytes[c][:, t, :], in_=w_v[:, t, c * BANK:(c + 1) * BANK])
+        def load_planes(c, t0, t1):
+            nc.sync.dma_start(out=w_bytes[c][:, t0:t1, :], in_=w_v[:, t0:t1, c * BANK:(c + 1) * BANK])
+
+        load_planes(0, 0, 1)
+        load_planes(3, 0, 1)
+        load_planes(0, 1, 2)
+        load_planes(0, 2, 4)
+        load_planes(3, 1, 4)
         nc.sync.dma_start(out=x_sb[:, 0:2, :], in_=x_v[:, 0:2, :])
         load_w(1)
         nc.sync.dma_start(out=x_sb[:, 2:4, :], in_=x_v[:, 2:4, :])

@@ -272,14 +272,14 @@ def tile_hgcn_pb_kernel(tc, x, w_sp_bytes, w_sp_scale, out):
         copy_pair(True, 0, xts[0])
         interleave(False, W0)
         widen(False, W1)
+        widen(True, W2)
         quantize_w(W0)
         quantize_x(0)
-        interleave(True, W3)
         for g in (1, 2, 3):
             xts[g] = transpose_pair(g)
         copy_pair(True, 1, xts[1])
         interleave(False, W1)
-        widen(False, W2)
+        interleave(False, W3)
         quantize_w(W1)
         quantize_x(1)
         interleave(False, W2)

@@ -26,13 +26,26 @@ W0 = (0, 512)
 W1 = (512, 1024)
 W2 = (1024, 1536)
 W3 = (1536, 2048)
-N_STEPS = 4 * TILES
-B_START = 8
-EXP_FIRST = 2
-EXP_AFTER = 3
-FAC_DELAY = 0
-S_HELP = (25, 27, 29, 31)
-LAST_EXP = 27
+AHEAD = 4
+HEAD = "plain"
+WIDTHS = [1, 1, 2] + [2] * 12 + [1, 1, 1, 1]
+SPLIT = 128
+
+V_BANKS = {}
+XC2_ON_S = False
+LAG = 8
+S_ITEMS = [("sq", 0, 0), ("sq", 1, 0), ("sq", 0, 1), ("sq", 1, 1), ("sq", 2, 0), ("sq", 0, 3), ("sq", 0, 2),
+           ("norm", 0), ("sq", 1, 3), ("sq", 1, 2), ("exp", 0), ("norm", 1), ("sq", 2, 1), ("sq", 2, 3),
+           ("sq", 2, 2), ("exp", 1), ("norm", 2), ("sq", 3, 0), ("sq", 3, 1), ("sq", 3, 2), ("exp", 2),
+           ("sq", 3, 3), ("norm", 3), ("sq", 4, 0), ("sq", 4, 1), ("sq", 4, 2), ("exp", 3), ("sq", 4, 3),
+           ("norm", 4), ("sq", 5, 0), ("sq", 5, 1), ("sq", 5, 2), ("exp", 4), ("sq", 5, 3), ("norm", 5),
+           ("sq", 6, 0), ("sq", 6, 1), ("sq", 6, 2), ("exp", 5), ("sq", 6, 3), ("norm", 6), ("sq", 7, 0),
+           ("sq", 7, 1), ("sq", 7, 2), ("exp", 6), ("sq", 7, 3), ("norm", 7), ("out", 6, 1), ("out", 6, 3),
+           ("exp", 7), ("out", 7, 1), ("out", 7, 3)]
+V_ITEMS = [("xc", 2), ("xc", 3), ("xq", 2), ("xq", 3)]
+V_FACTORS = (0, 7)
+V_AFTER = {}
+FEED_OUT = {7: 4}
 
 
 def tile_hgcn_pb_kernel(tc, x, w_sp_bytes, w_sp_scale, out):
@@ -48,10 +61,10 @@ def tile_hgcn_pb_kernel(tc, x, w_sp_bytes, w_sp_scale, out):
         psum = ctx.enter_context(tc.psum_pool(name="psum", bufs=4))
 
         ident = keep.tile([P, P], F32, name="ident")
+        ident_bf = keep.tile([P, P], BF16, name="ident_bf")
         w_scale = keep.tile([P, 4], F32, name="w_scale")
         plus_minus = keep.tile([P, 2], F32, name="plus_minus")
-        half = keep.tile([P, 1], F32, name="half")
-        minus_half = keep.tile([P, 1], F32, name="minus_half")
+        exponents = keep.tile([P, 2], F32, name="exponents")
         warm = keep.tile([P, 1], F32, name="warm")
         w_bytes = []
         w_wide = []
@@ -69,12 +82,13 @@ def tile_hgcn_pb_kernel(tc, x, w_sp_bytes, w_sp_scale, out):
         sumsq = keep.tile([P, 4 * TILES], F32, name="sumsq")
         part = keep.tile([P, TILES], F32, name="part")
         normsq = keep.tile([P, TILES], F32, name="normsq")
-        radius = keep.tile([P, TILES], F32, name="radius")
-        inv_radius = keep.tile([P, TILES], F32, name="inv_radius")
+        roots = keep.tile([P, 2 * TILES], F32, name="roots")
         halves = keep.tile([P, 2 * TILES], F32, name="halves")
         factor = keep.tile([P, TILES], F32, name="factor")
-        inv_radius_first = keep.tile([P, 1], F32, name="inv_radius_first")
-        factor_first = keep.tile([P, 1], F32, name="factor_first")
+        factor_v = keep.tile([P, TILES], F32, name="factor_v")
+        stats = keep.tile([P, 24 * TILES], F32, name="stats")
+        mean_var = keep.tile([P, 2 * TILES], F32, name="mean_var")
+        second_moment = keep.tile([P, TILES], F32, name="second_moment")
 
         x_words = x_sb[:].rearrange("p j k -> p (j k)").bitcast(F32)
         xg_words = x_group[:].bitcast(F32)
@@ -93,17 +107,22 @@ def tile_hgcn_pb_kernel(tc, x, w_sp_bytes, w_sp_scale, out):
         load_planes(0, 2, 4)
         load_planes(3, 1, 4)
         nc.sync.dma_start(out=x_sb[:, 0:2, :], in_=x_v[:, 0:2, :])
-        load_w(1)
+        load_w(2 if HEAD == "pe2" else 1)
+        if HEAD == "pe2":
+            load_w(1)
         nc.sync.dma_start(out=x_sb[:, 2:4, :], in_=x_v[:, 2:4, :])
-        load_w(2)
+        if HEAD != "pe2":
+            load_w(2)
         nc.sync.dma_start(out=x_sb[:, 4:TILES, :], in_=x_v[:, 4:TILES, :])
 
-        nc.vector.memset(half[:], 0.5)
-        nc.vector.memset(minus_half[:], -0.5)
+        nc.vector.memset(exponents[:, 0:1], 0.5)
+        nc.vector.memset(exponents[:, 1:2], -0.5)
         nc.vector.memset(plus_minus[:, 0:1], 1.0)
         nc.vector.memset(plus_minus[:, 1:2], -1.0)
-        nc.scalar.activation(out=warm[:], in_=half[:], func=ACT.Exp)
+        nc.scalar.activation(out=warm[:], in_=exponents[:, 0:1], func=ACT.Exp)
         make_identity(nc, ident[:])
+        if HEAD == "pe2":
+            make_identity(nc, ident_bf[:])
 
         def widen(on_scalar, piece):
             c = piece[0] // BANK
@@ -127,6 +146,28 @@ def tile_hgcn_pb_kernel(tc, x, w_sp_bytes, w_sp_scale, out):
                 nc.scalar.copy(out=dst, in_=src)
             else:
                 nc.vector.tensor_copy(out=dst, in_=src)
+
+        def interleave_on_tensor(c):
+            halves_of_bank = []
+            for hh in range(2):
+                wi = psum.tile([P, 2 * BANK], BF16, name="wi", tag="sq")
+                for q in range(2):
+                    n0 = 256 * hh + 128 * q
+                    nc.tensor.matmul(
+                        out=wi[:, BANK * q:BANK * (q + 1)].rearrange("p (n t) -> p n t", t=4),
+                        lhsT=ident_bf[:],
+                        rhs=w_wide[c][:, :, n0:n0 + 128].rearrange("p t n -> p n t"),
+                        start=True, stop=True,
+                    )
+                halves_of_bank.append(wi)
+            return halves_of_bank
+
+        def copy_interleaved(on_scalar, c, hh, wi):
+            lo = 4 * (BANK * c + 256 * hh)
+            if on_scalar:
+                nc.scalar.copy(out=w_group[:, lo:lo + 2 * BANK], in_=wi[:])
+            else:
+                nc.vector.tensor_copy(out=w_group[:, lo:lo + 2 * BANK], in_=wi[:])
 
         def quantize_w(piece):
             n0, n1 = piece
@@ -164,10 +205,8 @@ def tile_hgcn_pb_kernel(tc, x, w_sp_bytes, w_sp_scale, out):
                 in_=x_group[:, 1024 * g:1024 * (g + 1)],
             )
 
-        acc = {}
-
-        def product(i, c, stream):
-            bank = psum.tile([P, BANK], F32, name="acc_" + stream, tag=stream)
+        def product(i, c, tag):
+            bank = psum.tile([P, BANK], F32, name="acc_" + tag, tag=tag)
             nc.tensor.matmul_mx(
                 out=bank[:],
                 lhsT=x_codes[:, P * i:P * (i + 1)].bitcast(FP8X4),
@@ -177,144 +216,233 @@ def tile_hgcn_pb_kernel(tc, x, w_sp_bytes, w_sp_scale, out):
                 start=True,
                 stop=True,
             )
-            acc[(stream, i, c)] = bank
+            return bank
 
-        def square_sum(i, c, pos):
+        def square_sum(bank, i, pos):
             junk = scrap.tile([P, BANK], BF16, name="junk")
             nc.scalar.activation(
-                out=junk[:], in_=acc[("sq", i, c)][:], func=ACT.Square,
+                out=junk[:], in_=bank[:], func=ACT.Square,
                 accum_out=sumsq[:, 4 * i + pos:4 * i + pos + 1],
             )
 
+        def take_roots(i):
+            nc.gpsimd.tensor_tensor(
+                out=roots[:, 2 * i:2 * i + 2], in0=normsq[:, i:i + 1].to_broadcast([P, 2]), in1=exponents[:], op=ALU.pow,
+            )
+
         def norm(i):
+            assert V_BANKS.get(i, 0) == 0 or i in mom_done, ("moment not made", i)
             s = 4 * i
-            nc.gpsimd.tensor_scalar(
-                out=part[:, i:i + 1], in0=sumsq[:, s:s + 1],
-                scalar1=sumsq[:, s + 1:s + 2], scalar2=sumsq[:, s + 2:s + 3],
-                op0=ALU.add, op1=ALU.add,
-            )
-            nc.gpsimd.tensor_scalar(
-                out=normsq[:, i:i + 1], in0=sumsq[:, s + 3:s + 4],
-                scalar1=part[:, i:i + 1], scalar2=EPS * EPS,
-                op0=ALU.add, op1=ALU.max,
-            )
-            nc.gpsimd.tensor_tensor(out=radius[:, i:i + 1], in0=normsq[:, i:i + 1], in1=half[:], op=ALU.pow)
-            if i > 0:
-                nc.gpsimd.tensor_tensor(out=inv_radius[:, i:i + 1], in0=normsq[:, i:i + 1], in1=minus_half[:], op=ALU.pow)
+            if V_BANKS.get(i, 0) == 4:
+                nc.gpsimd.tensor_scalar(
+                    out=normsq[:, i:i + 1], in0=second_moment[:, i:i + 1],
+                    scalar1=float(D), scalar2=EPS * EPS, op0=ALU.mult, op1=ALU.max,
+                )
+            elif V_BANKS.get(i, 0) == 2:
+                nc.gpsimd.tensor_scalar(
+                    out=part[:, i:i + 1], in0=second_moment[:, i:i + 1],
+                    scalar1=float(2 * BANK), scalar2=sumsq[:, s:s + 1], op0=ALU.mult, op1=ALU.add,
+                )
+                nc.gpsimd.tensor_scalar(
+                    out=normsq[:, i:i + 1], in0=sumsq[:, s + 1:s + 2],
+                    scalar1=part[:, i:i + 1], scalar2=EPS * EPS,
+                    op0=ALU.add, op1=ALU.max,
+                )
+            else:
+                nc.gpsimd.tensor_scalar(
+                    out=part[:, i:i + 1], in0=sumsq[:, s:s + 1],
+                    scalar1=sumsq[:, s + 1:s + 2], scalar2=sumsq[:, s + 2:s + 3],
+                    op0=ALU.add, op1=ALU.add,
+                )
+                nc.gpsimd.tensor_scalar(
+                    out=normsq[:, i:i + 1], in0=sumsq[:, s + 3:s + 4],
+                    scalar1=part[:, i:i + 1], scalar2=EPS * EPS,
+                    op0=ALU.add, op1=ALU.max,
+                )
+            take_roots(i)
 
         def exponentials(i):
             nc.scalar.activation(
                 out=halves[:, 2 * i:2 * i + 2], in_=plus_minus[:], func=ACT.Exp,
-                scale=radius[:, i:i + 1], bias=-math.log(2.0),
+                scale=roots[:, 2 * i:2 * i + 1], bias=-math.log(2.0),
                 accum_out=result[:, ROW * i:ROW * i + 1],
             )
 
         def factor_of(i):
-            return factor_first[:] if i == 0 else factor[:, i:i + 1]
+            return factor_v[:, i:i + 1] if i in V_FACTORS else factor[:, i:i + 1]
 
         def make_factor(i):
-            if i == 0:
-                nc.vector.reciprocal(out=inv_radius_first[:], in_=radius[:, 0:1])
-                nc.vector.tensor_scalar(
-                    out=factor_first[:], in0=halves[:, 0:1],
-                    scalar1=halves[:, 1:2], scalar2=inv_radius_first[:],
-                    op0=ALU.subtract, op1=ALU.mult,
-                )
-            else:
-                nc.gpsimd.tensor_scalar(
-                    out=factor[:, i:i + 1], in0=halves[:, 2 * i:2 * i + 1],
-                    scalar1=halves[:, 2 * i + 1:2 * i + 2], scalar2=inv_radius[:, i:i + 1],
-                    op0=ALU.subtract, op1=ALU.mult,
-                )
+            eng = nc.vector if i in V_FACTORS else nc.gpsimd
+            eng.tensor_scalar(
+                out=factor_of(i), in0=halves[:, 2 * i:2 * i + 1],
+                scalar1=halves[:, 2 * i + 1:2 * i + 2], scalar2=roots[:, 2 * i + 1:2 * i + 2],
+                op0=ALU.subtract, op1=ALU.mult,
+            )
 
-        def scale_out(on_scalar, i, c):
+        def scale_out(on_scalar, bank, i, c):
+            assert i in exp_done, ("factor not made", i, c)
             lo = ROW * i + 1 + BANK * c
             dst = result[:, lo:lo + BANK]
             if on_scalar:
-                nc.scalar.activation(out=dst, in_=acc[("out", i, c)][:], func=ACT.Copy, scale=factor_of(i))
+                nc.scalar.activation(out=dst, in_=bank[:], func=ACT.Copy, scale=factor_of(i))
             else:
-                nc.vector.tensor_scalar(out=dst, in0=acc[("out", i, c)][:], scalar1=factor_of(i), scalar2=None, op0=ALU.mult)
+                nc.vector.tensor_scalar(out=dst, in0=bank[:], scalar1=factor_of(i), scalar2=None, op0=ALU.mult)
 
         def store(lo, hi):
             nc.sync.dma_start(out=out_v[:, lo:hi], in_=result[:, lo:hi])
 
-        a_order = [(0, 0), (1, 0), (0, 1), (1, 1), (2, 0), (0, 3), (0, 2), (1, 3), (1, 2), (2, 1), (2, 3), (2, 2)]
-        for i in range(3, TILES):
+        pieces = []
+        b = 0
+        for width in WIDTHS:
+            pieces.append((b, b + width - 1, BANK * b, BANK * (b + width) if b + width < 32 else TILES * ROW))
+            b += width
+
+        s_helped = [(it[1], it[2]) for it in S_ITEMS if it[0] == "out"]
+        v_items = list(V_ITEMS)
+        for i in range(TILES):
             for c in range(4):
-                a_order.append((i, c))
-        seen = {}
-        pos_of = []
-        last_step = {}
-        for n in range(N_STEPS):
-            i = a_order[n][0]
-            pos_of.append(seen.get(i, 0))
-            seen[i] = seen.get(i, 0) + 1
-            last_step[i] = n
-        exp_at = {}
-        fac_at = {}
-        for i in range(TILES - 1):
-            k = last_step[i] + (EXP_FIRST if i == 0 else EXP_AFTER)
-            exp_at[k] = i
-            fac_at[k + (0 if i == 0 else FAC_DELAY)] = i
-        cuts = {0: [(0, 512)], 1: [(512, 1024)], 3: [(1024, 2048)]}
-        for i in range(1, TILES - 1):
-            for h in range(2):
-                cuts[4 * i + 1 + 2 * h] = [(D * i + 1024 * h, D * i + 1024 * (h + 1))]
-        for c in range(3):
-            cuts[4 * (TILES - 1) + c] = [(D * (TILES - 1) + BANK * c, D * (TILES - 1) + BANK * (c + 1))]
-        cuts[N_STEPS - 1] = [(D * (TILES - 1) + BANK * 3, TILES * ROW)]
+                if (i, c) not in s_helped:
+                    v_items.append(("out", i, c))
+                for extra in V_AFTER.get((i, c), []):
+                    v_items.append(extra)
 
         ctx.enter_context(tc.manual_schedule())
         xts = {}
-        xts[0] = transpose_pair(0)
-        widen(False, W0)
-        widen(True, W3)
-        copy_pair(True, 0, xts[0])
-        interleave(False, W0)
-        widen(False, W1)
-        widen(True, W2)
-        quantize_w(W0)
-        quantize_x(0)
-        for g in (1, 2, 3):
-            xts[g] = transpose_pair(g)
-        copy_pair(True, 1, xts[1])
-        interleave(False, W1)
-        interleave(False, W3)
-        quantize_w(W1)
-        quantize_x(1)
-        interleave(False, W2)
-        quantize_w(W3)
-        quantize_w(W2)
-        for n in range(4):
-            product(a_order[n][0], a_order[n][1], "sq")
-        m = 0
-        for n in range(N_STEPS + B_START + 1):
-            if n < N_STEPS:
-                i, c = a_order[n]
-                square_sum(i, c, pos_of[n])
-                if n + 4 < N_STEPS:
-                    product(a_order[n + 4][0], a_order[n + 4][1], "sq")
-            if n in exp_at:
-                exponentials(exp_at[n])
-            if n in fac_at:
-                make_factor(fac_at[n])
-            if n < N_STEPS and last_step[a_order[n][0]] == n:
-                norm(a_order[n][0])
-            if n == 1:
-                copy_pair(False, 2, xts[2])
-                copy_pair(False, 3, xts[3])
-                quantize_x(2)
-                quantize_x(3)
-            if n == B_START:
-                for c in range(4):
-                    product(0, c, "out")
-            if n > B_START:
-                scale_out(m in S_HELP, m // 4, m % 4)
-                if m + 4 < N_STEPS:
-                    product((m + 4) // 4, (m + 4) % 4, "out")
-                for lo, hi in cuts.get(m, []):
+        needs = ("sq", "out", "bn")
+        streams = {"sq": [it for it in S_ITEMS if it[0] in needs], "out": [it for it in v_items if it[0] in needs]}
+        made = {"sq": 0, "out": 0}
+        banks = {}
+        seen = {}
+        bn_seen = {}
+        mom_done = set()
+        done_banks = set()
+        stored = set()
+        exp_done = set()
+
+        def feed(tag):
+            if made[tag] < len(streams[tag]):
+                it = streams[tag][made[tag]]
+                banks[(tag,) + it] = product(it[1], it[2], tag)
+                made[tag] += 1
+
+        def flush():
+            for q in range(len(pieces)):
+                b0, b1, lo, hi = pieces[q]
+                if q not in stored and all(b in done_banks for b in range(max(b0 - 1, 0), b1 + 1)) and (b0 // 4) in exp_done:
                     store(lo, hi)
-                if m == LAST_EXP:
-                    exponentials(TILES - 1)
-                    make_factor(TILES - 1)
-                m += 1
+                    stored.add(q)
+
+        def run(on_scalar, it):
+            tag = "sq" if on_scalar else "out"
+            kind = it[0]
+            if kind == "sq":
+                i = it[1]
+                square_sum(banks[(tag,) + it], i, seen.get(i, 0))
+                seen[i] = seen.get(i, 0) + 1
+                feed(tag)
+            elif kind == "norm":
+                norm(it[1])
+            elif kind == "exp":
+                exponentials(it[1])
+                exp_done.add(it[1])
+                make_factor(it[1])
+            elif kind == "out":
+                scale_out(on_scalar, banks[(tag,) + it], it[1], it[2])
+                done_banks.add(4 * it[1] + it[2])
+                feed(tag)
+                flush()
+            elif kind == "bn":
+                i = it[1]
+                k = bn_seen.get(i, 0)
+                bn_seen[i] = k + 1
+                nc.vector.bn_stats(out=stats[:, 24 * i + 6 * k:24 * i + 6 * k + 6], in_=banks[(tag,) + it][:])
+                feed(tag)
+            elif kind == "mom":
+                i = it[1]
+                mom_done.add(i)
+                nc.vector.bn_aggr(out=mean_var[:, 2 * i:2 * i + 2], in_=stats[:, 24 * i:24 * i + 6 * V_BANKS[i]])
+                nc.vector.scalar_tensor_tensor(
+                    out=second_moment[:, i:i + 1], in0=mean_var[:, 2 * i:2 * i + 1], scalar=mean_var[:, 2 * i:2 * i + 1],
+                    in1=mean_var[:, 2 * i + 1:2 * i + 2], op0=ALU.mult, op1=ALU.add,
+                )
+            elif kind == "xt":
+                xts[it[1]] = transpose_pair(it[1])
+            elif kind == "xc":
+                copy_pair(on_scalar, it[1], xts[it[1]])
+            elif kind == "xq":
+                quantize_x(it[1])
+
+        if HEAD == "plain":
+            xts[0] = transpose_pair(0)
+            widen(False, W0)
+            widen(True, W3)
+            copy_pair(True, 0, xts[0])
+            interleave(False, W0)
+            widen(False, W1)
+            widen(True, W2)
+            quantize_w(W0)
+            quantize_x(0)
+            for g in (1, 2, 3):
+                xts[g] = transpose_pair(g)
+            copy_pair(True, 1, xts[1])
+            if XC2_ON_S:
+                copy_pair(True, 2, xts[2])
+            interleave(False, W1)
+            interleave(False, W3)
+            quantize_w(W1)
+            quantize_x(1)
+            if SPLIT:
+                interleave(True, (1536 - SPLIT, 1536))
+            interleave(False, (1024, 1536 - SPLIT))
+            quantize_w(W3)
+            quantize_w(W2)
+            for q in range(AHEAD):
+                feed("sq")
+        else:
+            xts[0] = transpose_pair(0)
+            widen(False, W0)
+            widen(True, W3)
+            copy_pair(True, 0, xts[0])
+            interleave(False, W0)
+            wi3 = interleave_on_tensor(3)
+            widen(False, W2)
+            wi2 = interleave_on_tensor(2)
+            copy_interleaved(True, 3, 0, wi3[0])
+            copy_interleaved(True, 3, 1, wi3[1])
+            widen(False, W1)
+            quantize_w(W0)
+            quantize_x(0)
+            copy_interleaved(True, 2, 0, wi2[0])
+            copy_interleaved(True, 2, 1, wi2[1])
+            feed("sq")
+            feed("sq")
+            xts[1] = transpose_pair(1)
+            interleave(False, W1)
+            copy_pair(True, 1, xts[1])
+            quantize_w(W3)
+            quantize_w(W2)
+            feed("sq")
+            feed("sq")
+            quantize_x(1)
+            quantize_w(W1)
+        state = {"v": 0, "vb": 0}
+
+        def advance(target):
+            while state["v"] < len(v_items) and state["vb"] < target:
+                it = v_items[state["v"]]
+                if it[0] == "out" and it[1] not in exp_done:
+                    return
+                if it[0] in needs:
+                    state["vb"] += 1
+                run(False, it)
+                state["v"] += 1
+
+        sb = 0
+        for n in range(len(S_ITEMS)):
+            run(True, S_ITEMS[n])
+            for q in range(FEED_OUT.get(n, 0)):
+                feed("out")
+            if S_ITEMS[n][0] in needs:
+                sb += 1
+                advance(sb - LAG)
+        advance(10 ** 6)

@@ -18,34 +18,27 @@ K = 512
 D = 2048
 TILES = 8
 BANK = 512
+BANKS = D // BANK
 ROW = D + 1
 EPS = 1e-6
 FLOPS = 2 * 1024 * K * D
 
-W0 = (0, 512)
-W1 = (512, 1024)
-W2 = (1024, 1536)
-W3 = (1536, 2048)
 AHEAD = 4
-HEAD = "plain"
-WIDTHS = [1, 1, 2] + [2] * 12 + [1, 1, 1, 1]
-SPLIT = 128
 
-V_BANKS = {}
-XC2_ON_S = False
+SCALAR_COLUMNS = 128
+
+FIRST_SQUARES = ((0, 0), (1, 0), (0, 1), (1, 1), (2, 0), (0, 3), (0, 2), (1, 3), (1, 2), (2, 1), (2, 3), (2, 2))
+
+EXP_BEHIND_FIRST = 2
+EXP_BEHIND = 3
+
+SCALAR_SCALES = ((6, 1), (6, 3), (7, 1), (7, 3))
+
 LAG = 8
-S_ITEMS = [("sq", 0, 0), ("sq", 1, 0), ("sq", 0, 1), ("sq", 1, 1), ("sq", 2, 0), ("sq", 0, 3), ("sq", 0, 2),
-           ("norm", 0), ("sq", 1, 3), ("sq", 1, 2), ("exp", 0), ("norm", 1), ("sq", 2, 1), ("sq", 2, 3),
-           ("sq", 2, 2), ("exp", 1), ("norm", 2), ("sq", 3, 0), ("sq", 3, 1), ("sq", 3, 2), ("exp", 2),
-           ("sq", 3, 3), ("norm", 3), ("sq", 4, 0), ("sq", 4, 1), ("sq", 4, 2), ("exp", 3), ("sq", 4, 3),
-           ("norm", 4), ("sq", 5, 0), ("sq", 5, 1), ("sq", 5, 2), ("exp", 4), ("sq", 5, 3), ("norm", 5),
-           ("sq", 6, 0), ("sq", 6, 1), ("sq", 6, 2), ("exp", 5), ("sq", 6, 3), ("norm", 6), ("sq", 7, 0),
-           ("sq", 7, 1), ("sq", 7, 2), ("exp", 6), ("sq", 7, 3), ("norm", 7), ("out", 6, 1), ("out", 6, 3),
-           ("exp", 7), ("out", 7, 1), ("out", 7, 3)]
-V_ITEMS = [("xc", 2), ("xc", 3), ("xq", 2), ("xq", 3)]
-V_FACTORS = (0, 7)
-V_AFTER = {}
-FEED_OUT = {7: 4}
+
+VECTOR_FACTORS = (0, TILES - 1)
+
+STORE_BANKS = (1, 1, 2) + (2,) * 12 + (1, 1, 1, 1)
 
 
 def tile_hgcn_pb_kernel(tc, x, w_sp_bytes, w_sp_scale, out):
@@ -58,17 +51,16 @@ def tile_hgcn_pb_kernel(tc, x, w_sp_bytes, w_sp_scale, out):
     with ExitStack() as ctx:
         keep = ctx.enter_context(tc.tile_pool(name="keep", bufs=1))
         scrap = ctx.enter_context(tc.tile_pool(name="scrap", bufs=2))
-        psum = ctx.enter_context(tc.psum_pool(name="psum", bufs=4))
+        psum = ctx.enter_context(tc.psum_pool(name="psum", bufs=AHEAD))
 
         ident = keep.tile([P, P], F32, name="ident")
-        ident_bf = keep.tile([P, P], BF16, name="ident_bf")
         w_scale = keep.tile([P, 4], F32, name="w_scale")
         plus_minus = keep.tile([P, 2], F32, name="plus_minus")
         exponents = keep.tile([P, 2], F32, name="exponents")
         warm = keep.tile([P, 1], F32, name="warm")
         w_bytes = []
         w_wide = []
-        for c in range(4):
+        for c in range(BANKS):
             w_bytes.append(keep.tile([P, 4, BANK], U8, name="w_bytes%d" % c))
             w_wide.append(keep.tile([P, 4, BANK], BF16, name="w_wide%d" % c))
         w_group = keep.tile([P, 4 * D], BF16, name="w_group", align_bytes=64)
@@ -79,41 +71,34 @@ def tile_hgcn_pb_kernel(tc, x, w_sp_bytes, w_sp_scale, out):
         x_codes = keep.tile([P, TILES * P], U32, name="x_codes", align_bytes=64)
         x_scales = keep.tile([P, TILES * P], U8, name="x_scales", align_bytes=64)
         result = keep.tile([P, TILES * ROW], F32, name="result")
-        sumsq = keep.tile([P, 4 * TILES], F32, name="sumsq")
+        sumsq = keep.tile([P, BANKS * TILES], F32, name="sumsq")
         part = keep.tile([P, TILES], F32, name="part")
         normsq = keep.tile([P, TILES], F32, name="normsq")
         roots = keep.tile([P, 2 * TILES], F32, name="roots")
         halves = keep.tile([P, 2 * TILES], F32, name="halves")
         factor = keep.tile([P, TILES], F32, name="factor")
         factor_v = keep.tile([P, TILES], F32, name="factor_v")
-        stats = keep.tile([P, 24 * TILES], F32, name="stats")
-        mean_var = keep.tile([P, 2 * TILES], F32, name="mean_var")
-        second_moment = keep.tile([P, TILES], F32, name="second_moment")
 
         x_words = x_sb[:].rearrange("p j k -> p (j k)").bitcast(F32)
         xg_words = x_group[:].bitcast(F32)
 
-        nc.scalar.dma_start(out=w_scale[:], in_=s_v)
-
-        def load_w(c):
-            nc.sync.dma_start(out=w_bytes[c][:], in_=w_v[:, :, c * BANK:(c + 1) * BANK])
-
-        def load_planes(c, t0, t1):
+        def load_w(c, t0, t1):
             nc.sync.dma_start(out=w_bytes[c][:, t0:t1, :], in_=w_v[:, t0:t1, c * BANK:(c + 1) * BANK])
 
-        load_planes(0, 0, 1)
-        load_planes(3, 0, 1)
-        load_planes(0, 1, 2)
-        load_planes(0, 2, 4)
-        load_planes(3, 1, 4)
-        nc.sync.dma_start(out=x_sb[:, 0:2, :], in_=x_v[:, 0:2, :])
-        load_w(2 if HEAD == "pe2" else 1)
-        if HEAD == "pe2":
-            load_w(1)
-        nc.sync.dma_start(out=x_sb[:, 2:4, :], in_=x_v[:, 2:4, :])
-        if HEAD != "pe2":
-            load_w(2)
-        nc.sync.dma_start(out=x_sb[:, 4:TILES, :], in_=x_v[:, 4:TILES, :])
+        def load_x(j0, j1):
+            nc.sync.dma_start(out=x_sb[:, j0:j1, :], in_=x_v[:, j0:j1, :])
+
+        nc.scalar.dma_start(out=w_scale[:], in_=s_v)
+        load_w(0, 0, 1)
+        load_w(3, 0, 1)
+        load_w(0, 1, 2)
+        load_w(0, 2, 4)
+        load_w(3, 1, 4)
+        load_x(0, 2)
+        load_w(1, 0, 4)
+        load_x(2, 4)
+        load_w(2, 0, 4)
+        load_x(4, TILES)
 
         nc.vector.memset(exponents[:, 0:1], 0.5)
         nc.vector.memset(exponents[:, 1:2], -0.5)
@@ -121,78 +106,48 @@ def tile_hgcn_pb_kernel(tc, x, w_sp_bytes, w_sp_scale, out):
         nc.vector.memset(plus_minus[:, 1:2], -1.0)
         nc.scalar.activation(out=warm[:], in_=exponents[:, 0:1], func=ACT.Exp)
         make_identity(nc, ident[:])
-        if HEAD == "pe2":
-            make_identity(nc, ident_bf[:])
 
-        def widen(on_scalar, piece):
-            c = piece[0] // BANK
-            a = piece[0] - c * BANK
-            b = piece[1] - c * BANK
+        def widen(on_scalar, c):
             for t in range(4):
-                src = w_bytes[c][:, t, a:b].bitcast(FP8)
-                dst = w_wide[c][:, t, a:b]
+                src = w_bytes[c][:, t, :].bitcast(FP8)
+                dst = w_wide[c][:, t, :]
                 if on_scalar:
                     nc.scalar.activation(out=dst, in_=src, func=ACT.Copy, scale=w_scale[:, t:t + 1])
                 else:
                     nc.vector.tensor_scalar(out=dst, in0=src, scalar1=w_scale[:, t:t + 1], scalar2=None, op0=ALU.mult)
 
-        def interleave(on_scalar, piece):
-            c = piece[0] // BANK
-            a = piece[0] - c * BANK
-            b = piece[1] - c * BANK
-            src = w_wide[c][:, :, a:b].rearrange("p t (g i) -> p g t i", i=4)
-            dst = w_group[:, 4 * piece[0]:4 * piece[1]].rearrange("p (g i t) -> p g t i", i=4, t=4)
+        def interleave(on_scalar, n0, n1):
+            c = n0 // BANK
+            src = w_wide[c][:, :, n0 - c * BANK:n1 - c * BANK].rearrange("p t (g i) -> p g t i", i=4)
+            dst = w_group[:, 4 * n0:4 * n1].rearrange("p (g i t) -> p g t i", i=4, t=4)
             if on_scalar:
                 nc.scalar.copy(out=dst, in_=src)
             else:
                 nc.vector.tensor_copy(out=dst, in_=src)
 
-        def interleave_on_tensor(c):
-            halves_of_bank = []
-            for hh in range(2):
-                wi = psum.tile([P, 2 * BANK], BF16, name="wi", tag="sq")
-                for q in range(2):
-                    n0 = 256 * hh + 128 * q
-                    nc.tensor.matmul(
-                        out=wi[:, BANK * q:BANK * (q + 1)].rearrange("p (n t) -> p n t", t=4),
-                        lhsT=ident_bf[:],
-                        rhs=w_wide[c][:, :, n0:n0 + 128].rearrange("p t n -> p n t"),
-                        start=True, stop=True,
-                    )
-                halves_of_bank.append(wi)
-            return halves_of_bank
-
-        def copy_interleaved(on_scalar, c, hh, wi):
-            lo = 4 * (BANK * c + 256 * hh)
-            if on_scalar:
-                nc.scalar.copy(out=w_group[:, lo:lo + 2 * BANK], in_=wi[:])
-            else:
-                nc.vector.tensor_copy(out=w_group[:, lo:lo + 2 * BANK], in_=wi[:])
-
-        def quantize_w(piece):
-            n0, n1 = piece
+        def quantize_w(c):
+            n0 = c * BANK
+            n1 = n0 + BANK
             nc.vector.quantize_mx(
                 out=w_codes[:, n0:n1].bitcast(FP8X4),
                 scales=w_scales[:, n0:n1],
                 in_=w_group[:, 4 * n0:4 * n1],
             )
 
-        def transpose_pair(g):
-            xt = psum.tile([P, BANK], F32, name="xt", tag="out")
+        x_banks = {}
+
+        def transpose_x(g):
+            bank = psum.tile([P, BANK], F32, name="xt", tag="vector")
             for jj in range(2):
                 for u in range(2):
                     j = 2 * g + jj
                     s = 2 * jj + u
-                    nc.tensor.transpose(
-                        xt[:, s * P:(s + 1) * P],
-                        x_words[:, 256 * j + u:256 * (j + 1):2],
-                        ident[:],
-                    )
-            return xt
+                    nc.tensor.transpose(bank[:, s * P:(s + 1) * P], x_words[:, 256 * j + u:256 * (j + 1):2], ident[:])
+            x_banks[g] = bank
 
-        def copy_pair(on_scalar, g, xt):
+        def copy_x(on_scalar, g):
             dst = xg_words[:, BANK * g:BANK * (g + 1)].rearrange("p (j r u) -> p j r u", j=2, u=2)
-            src = xt[:].rearrange("p (j u r) -> p j r u", j=2, u=2)
+            src = x_banks[g][:].rearrange("p (j u r) -> p j r u", j=2, u=2)
             if on_scalar:
                 nc.scalar.copy(out=dst, in_=src)
             else:
@@ -205,8 +160,8 @@ def tile_hgcn_pb_kernel(tc, x, w_sp_bytes, w_sp_scale, out):
                 in_=x_group[:, 1024 * g:1024 * (g + 1)],
             )
 
-        def product(i, c, tag):
-            bank = psum.tile([P, BANK], F32, name="acc_" + tag, tag=tag)
+        def product(i, c, stream):
+            bank = psum.tile([P, BANK], F32, name="acc_" + stream, tag=stream)
             nc.tensor.matmul_mx(
                 out=bank[:],
                 lhsT=x_codes[:, P * i:P * (i + 1)].bitcast(FP8X4),
@@ -222,44 +177,24 @@ def tile_hgcn_pb_kernel(tc, x, w_sp_bytes, w_sp_scale, out):
             junk = scrap.tile([P, BANK], BF16, name="junk")
             nc.scalar.activation(
                 out=junk[:], in_=bank[:], func=ACT.Square,
-                accum_out=sumsq[:, 4 * i + pos:4 * i + pos + 1],
-            )
-
-        def take_roots(i):
-            nc.gpsimd.tensor_tensor(
-                out=roots[:, 2 * i:2 * i + 2], in0=normsq[:, i:i + 1].to_broadcast([P, 2]), in1=exponents[:], op=ALU.pow,
+                accum_out=sumsq[:, BANKS * i + pos:BANKS * i + pos + 1],
             )
 
         def norm(i):
-            assert V_BANKS.get(i, 0) == 0 or i in mom_done, ("moment not made", i)
-            s = 4 * i
-            if V_BANKS.get(i, 0) == 4:
-                nc.gpsimd.tensor_scalar(
-                    out=normsq[:, i:i + 1], in0=second_moment[:, i:i + 1],
-                    scalar1=float(D), scalar2=EPS * EPS, op0=ALU.mult, op1=ALU.max,
-                )
-            elif V_BANKS.get(i, 0) == 2:
-                nc.gpsimd.tensor_scalar(
-                    out=part[:, i:i + 1], in0=second_moment[:, i:i + 1],
-                    scalar1=float(2 * BANK), scalar2=sumsq[:, s:s + 1], op0=ALU.mult, op1=ALU.add,
-                )
-                nc.gpsimd.tensor_scalar(
-                    out=normsq[:, i:i + 1], in0=sumsq[:, s + 1:s + 2],
-                    scalar1=part[:, i:i + 1], scalar2=EPS * EPS,
-                    op0=ALU.add, op1=ALU.max,
-                )
-            else:
-                nc.gpsimd.tensor_scalar(
-                    out=part[:, i:i + 1], in0=sumsq[:, s:s + 1],
-                    scalar1=sumsq[:, s + 1:s + 2], scalar2=sumsq[:, s + 2:s + 3],
-                    op0=ALU.add, op1=ALU.add,
-                )
-                nc.gpsimd.tensor_scalar(
-                    out=normsq[:, i:i + 1], in0=sumsq[:, s + 3:s + 4],
-                    scalar1=part[:, i:i + 1], scalar2=EPS * EPS,
-                    op0=ALU.add, op1=ALU.max,
-                )
-            take_roots(i)
+            s = BANKS * i
+            nc.gpsimd.tensor_scalar(
+                out=part[:, i:i + 1], in0=sumsq[:, s:s + 1],
+                scalar1=sumsq[:, s + 1:s + 2], scalar2=sumsq[:, s + 2:s + 3],
+                op0=ALU.add, op1=ALU.add,
+            )
+            nc.gpsimd.tensor_scalar(
+                out=normsq[:, i:i + 1], in0=sumsq[:, s + 3:s + 4],
+                scalar1=part[:, i:i + 1], scalar2=EPS * EPS,
+                op0=ALU.add, op1=ALU.max,
+            )
+            nc.gpsimd.tensor_tensor(
+                out=roots[:, 2 * i:2 * i + 2], in0=normsq[:, i:i + 1].to_broadcast([P, 2]), in1=exponents[:], op=ALU.pow,
+            )
 
         def exponentials(i):
             nc.scalar.activation(
@@ -269,18 +204,17 @@ def tile_hgcn_pb_kernel(tc, x, w_sp_bytes, w_sp_scale, out):
             )
 
         def factor_of(i):
-            return factor_v[:, i:i + 1] if i in V_FACTORS else factor[:, i:i + 1]
+            return factor_v[:, i:i + 1] if i in VECTOR_FACTORS else factor[:, i:i + 1]
 
         def make_factor(i):
-            eng = nc.vector if i in V_FACTORS else nc.gpsimd
-            eng.tensor_scalar(
+            engine = nc.vector if i in VECTOR_FACTORS else nc.gpsimd
+            engine.tensor_scalar(
                 out=factor_of(i), in0=halves[:, 2 * i:2 * i + 1],
                 scalar1=halves[:, 2 * i + 1:2 * i + 2], scalar2=roots[:, 2 * i + 1:2 * i + 2],
                 op0=ALU.subtract, op1=ALU.mult,
             )
 
         def scale_out(on_scalar, bank, i, c):
-            assert i in exp_done, ("factor not made", i, c)
             lo = ROW * i + 1 + BANK * c
             dst = result[:, lo:lo + BANK]
             if on_scalar:
@@ -288,161 +222,133 @@ def tile_hgcn_pb_kernel(tc, x, w_sp_bytes, w_sp_scale, out):
             else:
                 nc.vector.tensor_scalar(out=dst, in0=bank[:], scalar1=factor_of(i), scalar2=None, op0=ALU.mult)
 
-        def store(lo, hi):
-            nc.sync.dma_start(out=out_v[:, lo:hi], in_=result[:, lo:hi])
-
         pieces = []
-        b = 0
-        for width in WIDTHS:
-            pieces.append((b, b + width - 1, BANK * b, BANK * (b + width) if b + width < 32 else TILES * ROW))
-            b += width
-
-        s_helped = [(it[1], it[2]) for it in S_ITEMS if it[0] == "out"]
-        v_items = list(V_ITEMS)
-        for i in range(TILES):
-            for c in range(4):
-                if (i, c) not in s_helped:
-                    v_items.append(("out", i, c))
-                for extra in V_AFTER.get((i, c), []):
-                    v_items.append(extra)
-
-        ctx.enter_context(tc.manual_schedule())
-        xts = {}
-        needs = ("sq", "out", "bn")
-        streams = {"sq": [it for it in S_ITEMS if it[0] in needs], "out": [it for it in v_items if it[0] in needs]}
-        made = {"sq": 0, "out": 0}
-        banks = {}
-        seen = {}
-        bn_seen = {}
-        mom_done = set()
-        done_banks = set()
+        b0 = 0
+        for width in STORE_BANKS:
+            b1 = b0 + width - 1
+            pieces.append((b0, b1, BANK * b0, BANK * (b1 + 1) if b1 < BANKS * TILES - 1 else TILES * ROW))
+            b0 += width
+        scaled = set()
+        exp_written = set()
         stored = set()
-        exp_done = set()
 
-        def feed(tag):
-            if made[tag] < len(streams[tag]):
-                it = streams[tag][made[tag]]
-                banks[(tag,) + it] = product(it[1], it[2], tag)
-                made[tag] += 1
-
-        def flush():
+        def store_what_is_ready():
             for q in range(len(pieces)):
-                b0, b1, lo, hi = pieces[q]
-                if q not in stored and all(b in done_banks for b in range(max(b0 - 1, 0), b1 + 1)) and (b0 // 4) in exp_done:
-                    store(lo, hi)
+                first, last, lo, hi = pieces[q]
+                if q in stored or first // BANKS not in exp_written:
+                    continue
+                if all(b in scaled for b in range(max(first - 1, 0), last + 1)):
+                    nc.sync.dma_start(out=out_v[:, lo:hi], in_=result[:, lo:hi])
                     stored.add(q)
 
-        def run(on_scalar, it):
-            tag = "sq" if on_scalar else "out"
-            kind = it[0]
-            if kind == "sq":
-                i = it[1]
-                square_sum(banks[(tag,) + it], i, seen.get(i, 0))
-                seen[i] = seen.get(i, 0) + 1
-                feed(tag)
-            elif kind == "norm":
-                norm(it[1])
-            elif kind == "exp":
-                exponentials(it[1])
-                exp_done.add(it[1])
-                make_factor(it[1])
-            elif kind == "out":
-                scale_out(on_scalar, banks[(tag,) + it], it[1], it[2])
-                done_banks.add(4 * it[1] + it[2])
-                feed(tag)
-                flush()
-            elif kind == "bn":
-                i = it[1]
-                k = bn_seen.get(i, 0)
-                bn_seen[i] = k + 1
-                nc.vector.bn_stats(out=stats[:, 24 * i + 6 * k:24 * i + 6 * k + 6], in_=banks[(tag,) + it][:])
-                feed(tag)
-            elif kind == "mom":
-                i = it[1]
-                mom_done.add(i)
-                nc.vector.bn_aggr(out=mean_var[:, 2 * i:2 * i + 2], in_=stats[:, 24 * i:24 * i + 6 * V_BANKS[i]])
-                nc.vector.scalar_tensor_tensor(
-                    out=second_moment[:, i:i + 1], in0=mean_var[:, 2 * i:2 * i + 1], scalar=mean_var[:, 2 * i:2 * i + 1],
-                    in1=mean_var[:, 2 * i + 1:2 * i + 2], op0=ALU.mult, op1=ALU.add,
-                )
-            elif kind == "xt":
-                xts[it[1]] = transpose_pair(it[1])
-            elif kind == "xc":
-                copy_pair(on_scalar, it[1], xts[it[1]])
-            elif kind == "xq":
-                quantize_x(it[1])
+        squares = list(FIRST_SQUARES)
+        for i in range(3, TILES):
+            for c in range(BANKS):
+                squares.append((i, c))
+        last_square = {}
+        for n in range(len(squares)):
+            last_square[squares[n][0]] = n
+        scalar_list = []
+        for n in range(len(squares)):
+            i, c = squares[n]
+            scalar_list.append(("square", i, c))
+            for j in range(TILES - 1):
+                if n == last_square[j] + (EXP_BEHIND_FIRST if j == 0 else EXP_BEHIND):
+                    scalar_list.append(("exp", j))
+            if n == last_square[i]:
+                scalar_list.append(("norm", i))
+        for i, c in SCALAR_SCALES:
+            if i == TILES - 1 and ("exp", i) not in scalar_list:
+                scalar_list.append(("exp", i))
+            scalar_list.append(("scale", i, c))
 
-        if HEAD == "plain":
-            xts[0] = transpose_pair(0)
-            widen(False, W0)
-            widen(True, W3)
-            copy_pair(True, 0, xts[0])
-            interleave(False, W0)
-            widen(False, W1)
-            widen(True, W2)
-            quantize_w(W0)
-            quantize_x(0)
-            for g in (1, 2, 3):
-                xts[g] = transpose_pair(g)
-            copy_pair(True, 1, xts[1])
-            if XC2_ON_S:
-                copy_pair(True, 2, xts[2])
-            interleave(False, W1)
-            interleave(False, W3)
-            quantize_w(W1)
-            quantize_x(1)
-            if SPLIT:
-                interleave(True, (1536 - SPLIT, 1536))
-            interleave(False, (1024, 1536 - SPLIT))
-            quantize_w(W3)
-            quantize_w(W2)
-            for q in range(AHEAD):
-                feed("sq")
-        else:
-            xts[0] = transpose_pair(0)
-            widen(False, W0)
-            widen(True, W3)
-            copy_pair(True, 0, xts[0])
-            interleave(False, W0)
-            wi3 = interleave_on_tensor(3)
-            widen(False, W2)
-            wi2 = interleave_on_tensor(2)
-            copy_interleaved(True, 3, 0, wi3[0])
-            copy_interleaved(True, 3, 1, wi3[1])
-            widen(False, W1)
-            quantize_w(W0)
-            quantize_x(0)
-            copy_interleaved(True, 2, 0, wi2[0])
-            copy_interleaved(True, 2, 1, wi2[1])
-            feed("sq")
-            feed("sq")
-            xts[1] = transpose_pair(1)
-            interleave(False, W1)
-            copy_pair(True, 1, xts[1])
-            quantize_w(W3)
-            quantize_w(W2)
-            feed("sq")
-            feed("sq")
-            quantize_x(1)
-            quantize_w(W1)
-        state = {"v": 0, "vb": 0}
+        vector_list = []
+        for i in range(TILES):
+            for c in range(BANKS):
+                if (i, c) not in SCALAR_SCALES:
+                    vector_list.append(("scale", i, c))
+
+        reads_bank = ("square", "scale")
+        streams = {
+            "scalar": [item for item in scalar_list if item[0] in reads_bank],
+            "vector": [item for item in vector_list if item[0] in reads_bank],
+        }
+        made = {"scalar": 0, "vector": 0}
+        banks = {}
+        squares_done = {}
+
+        def next_product(stream):
+            if made[stream] < len(streams[stream]):
+                item = streams[stream][made[stream]]
+                banks[(stream,) + item] = product(item[1], item[2], stream)
+                made[stream] += 1
+
+        def run(on_scalar, item):
+            stream = "scalar" if on_scalar else "vector"
+            kind = item[0]
+            i = item[1]
+            if kind == "square":
+                square_sum(banks[(stream,) + item], i, squares_done.get(i, 0))
+                squares_done[i] = squares_done.get(i, 0) + 1
+                next_product(stream)
+            elif kind == "norm":
+                norm(i)
+            elif kind == "exp":
+                exponentials(i)
+                exp_written.add(i)
+                make_factor(i)
+            elif kind == "scale":
+                scale_out(on_scalar, banks[(stream,) + item], i, item[2])
+                scaled.add(BANKS * i + item[2])
+                next_product(stream)
+                store_what_is_ready()
+
+        ctx.enter_context(tc.manual_schedule())
+
+        transpose_x(0)
+        widen(False, 0)
+        widen(True, 3)
+        copy_x(True, 0)
+        interleave(False, 0, BANK)
+        widen(False, 1)
+        widen(True, 2)
+        quantize_w(0)
+        quantize_x(0)
+        for g in (1, 2, 3):
+            transpose_x(g)
+        copy_x(True, 1)
+        interleave(False, BANK, 2 * BANK)
+        interleave(False, 3 * BANK, 4 * BANK)
+        quantize_w(1)
+        quantize_x(1)
+        interleave(True, 3 * BANK - SCALAR_COLUMNS, 3 * BANK)
+        interleave(False, 2 * BANK, 3 * BANK - SCALAR_COLUMNS)
+        quantize_w(3)
+        quantize_w(2)
+        copy_x(False, 2)
+        copy_x(False, 3)
+        quantize_x(2)
+        quantize_x(3)
+
+        for q in range(AHEAD):
+            next_product("scalar")
+        written = {"vector": 0}
 
         def advance(target):
-            while state["v"] < len(v_items) and state["vb"] < target:
-                it = v_items[state["v"]]
-                if it[0] == "out" and it[1] not in exp_done:
+            while written["vector"] < min(target, len(vector_list)):
+                item = vector_list[written["vector"]]
+                if item[1] not in exp_written:
                     return
-                if it[0] in needs:
-                    state["vb"] += 1
-                run(False, it)
-                state["v"] += 1
+                run(False, item)
+                written["vector"] += 1
 
-        sb = 0
-        for n in range(len(S_ITEMS)):
-            run(True, S_ITEMS[n])
-            for q in range(FEED_OUT.get(n, 0)):
-                feed("out")
-            if S_ITEMS[n][0] in needs:
-                sb += 1
-                advance(sb - LAG)
-        advance(10 ** 6)
+        read_by_scalar = 0
+        for item in scalar_list:
+            run(True, item)
+            if item == ("norm", 0):
+                for q in range(AHEAD):
+                    next_product("vector")
+            if item[0] in reads_bank:
+                read_by_scalar += 1
+                advance(read_by_scalar - LAG)
+        advance(len(vector_list))

from contextlib import ExitStack
import math

import concourse.mybir as mybir
from concourse.masks import make_identity

F32 = mybir.dt.float32
BF16 = mybir.dt.bfloat16
U8 = mybir.dt.uint8
U32 = mybir.dt.uint32
FP8 = mybir.dt.float8_e4m3fn
FP8X4 = mybir.dt.float8_e4m3fn_x4
ACT = mybir.ActivationFunctionType
ALU = mybir.AluOpType

P = 128
K = 512
D = 2048
TILES = 8
BANK = 512
BANKS = D // BANK
ROW = D + 1
EPS = 1e-6
FLOPS = 2 * 1024 * K * D

AHEAD = 4

SCALAR_COLUMNS = 128

FIRST_SQUARES = ((0, 0), (1, 0), (0, 1), (1, 1), (2, 0), (0, 3), (0, 2), (1, 3), (1, 2), (2, 1), (2, 3), (2, 2))

EXP_BEHIND_FIRST = 2
EXP_BEHIND = 3

SCALAR_SCALES = ((6, 1), (6, 3), (7, 1), (7, 3))

LAG = 8

VECTOR_FACTORS = (0, TILES - 1)

STORE_BANKS = (1, 1, 2) + (2,) * 12 + (1, 1, 1, 1)


def tile_hgcn_pb_kernel(tc, x, w_sp_bytes, w_sp_scale, out):
    nc = tc.nc
    x_v = x.rearrange("b (q j) k -> (b q) j k", j=TILES)
    w_v = w_sp_bytes.rearrange("(p t) n -> p t n", t=4)
    s_v = w_sp_scale.rearrange("(p t) o -> p (t o)", t=4)
    out_v = out.rearrange("b (q j) c -> (b q) (j c)", j=TILES)

    with ExitStack() as ctx:
        keep = ctx.enter_context(tc.tile_pool(name="keep", bufs=1))
        scrap = ctx.enter_context(tc.tile_pool(name="scrap", bufs=2))
        psum = ctx.enter_context(tc.psum_pool(name="psum", bufs=AHEAD))

        ident = keep.tile([P, P], F32, name="ident")
        w_scale = keep.tile([P, 4], F32, name="w_scale")
        plus_minus = keep.tile([P, 2], F32, name="plus_minus")
        exponents = keep.tile([P, 2], F32, name="exponents")
        warm = keep.tile([P, 1], F32, name="warm")
        w_bytes = []
        w_wide = []
        for c in range(BANKS):
            w_bytes.append(keep.tile([P, 4, BANK], U8, name="w_bytes%d" % c))
            w_wide.append(keep.tile([P, 4, BANK], BF16, name="w_wide%d" % c))
        w_group = keep.tile([P, 4 * D], BF16, name="w_group", align_bytes=64)
        w_codes = keep.tile([P, D], U32, name="w_codes", align_bytes=64)
        w_scales = keep.tile([P, D], U8, name="w_scales", align_bytes=64)
        x_sb = keep.tile([P, TILES, K], BF16, name="x_sb")
        x_group = keep.tile([P, TILES * K], BF16, name="x_group", align_bytes=64)
        x_codes = keep.tile([P, TILES * P], U32, name="x_codes", align_bytes=64)
        x_scales = keep.tile([P, TILES * P], U8, name="x_scales", align_bytes=64)
        result = keep.tile([P, TILES * ROW], F32, name="result")
        sumsq = keep.tile([P, BANKS * TILES], F32, name="sumsq")
        part = keep.tile([P, TILES], F32, name="part")
        normsq = keep.tile([P, TILES], F32, name="normsq")
        roots = keep.tile([P, 2 * TILES], F32, name="roots")
        halves = keep.tile([P, 2 * TILES], F32, name="halves")
        factor = keep.tile([P, TILES], F32, name="factor")
        factor_v = keep.tile([P, TILES], F32, name="factor_v")

        x_words = x_sb[:].rearrange("p j k -> p (j k)").bitcast(F32)
        xg_words = x_group[:].bitcast(F32)

        def load_w(c, t0, t1):
            nc.sync.dma_start(out=w_bytes[c][:, t0:t1, :], in_=w_v[:, t0:t1, c * BANK:(c + 1) * BANK])

        def load_x(j0, j1):
            nc.sync.dma_start(out=x_sb[:, j0:j1, :], in_=x_v[:, j0:j1, :])

        nc.scalar.dma_start(out=w_scale[:], in_=s_v)
        load_w(0, 0, 1)
        load_w(3, 0, 1)
        load_w(0, 1, 2)
        load_w(0, 2, 4)
        load_w(3, 1, 4)
        load_x(0, 2)
        load_w(1, 0, 4)
        load_x(2, 4)
        load_w(2, 0, 4)
        load_x(4, TILES)

        nc.vector.memset(exponents[:, 0:1], 0.5)
        nc.vector.memset(exponents[:, 1:2], -0.5)
        nc.vector.memset(plus_minus[:, 0:1], 1.0)
        nc.vector.memset(plus_minus[:, 1:2], -1.0)
        nc.scalar.activation(out=warm[:], in_=exponents[:, 0:1], func=ACT.Exp)
        make_identity(nc, ident[:])

        def widen(on_scalar, c):
            for t in range(4):
                src = w_bytes[c][:, t, :].bitcast(FP8)
                dst = w_wide[c][:, t, :]
                if on_scalar:
                    nc.scalar.activation(out=dst, in_=src, func=ACT.Copy, scale=w_scale[:, t:t + 1])
                else:
                    nc.vector.tensor_scalar(out=dst, in0=src, scalar1=w_scale[:, t:t + 1], scalar2=None, op0=ALU.mult)

        def interleave(on_scalar, n0, n1):
            c = n0 // BANK
            src = w_wide[c][:, :, n0 - c * BANK:n1 - c * BANK].rearrange("p t (g i) -> p g t i", i=4)
            dst = w_group[:, 4 * n0:4 * n1].rearrange("p (g i t) -> p g t i", i=4, t=4)
            if on_scalar:
                nc.scalar.copy(out=dst, in_=src)
            else:
                nc.vector.tensor_copy(out=dst, in_=src)

        def quantize_w(c):
            n0 = c * BANK
            n1 = n0 + BANK
            nc.vector.quantize_mx(
                out=w_codes[:, n0:n1].bitcast(FP8X4),
                scales=w_scales[:, n0:n1],
                in_=w_group[:, 4 * n0:4 * n1],
            )

        x_banks = {}

        def transpose_x(g):
            bank = psum.tile([P, BANK], F32, name="xt", tag="vector")
            for jj in range(2):
                for u in range(2):
                    j = 2 * g + jj
                    s = 2 * jj + u
                    nc.tensor.transpose(bank[:, s * P:(s + 1) * P], x_words[:, 256 * j + u:256 * (j + 1):2], ident[:])
            x_banks[g] = bank

        def copy_x(on_scalar, g):
            dst = xg_words[:, BANK * g:BANK * (g + 1)].rearrange("p (j r u) -> p j r u", j=2, u=2)
            src = x_banks[g][:].rearrange("p (j u r) -> p j r u", j=2, u=2)
            if on_scalar:
                nc.scalar.copy(out=dst, in_=src)
            else:
                nc.vector.tensor_copy(out=dst, in_=src)

        def quantize_x(g):
            nc.vector.quantize_mx(
                out=x_codes[:, 256 * g:256 * (g + 1)].bitcast(FP8X4),
                scales=x_scales[:, 256 * g:256 * (g + 1)],
                in_=x_group[:, 1024 * g:1024 * (g + 1)],
            )

        def product(i, c, stream):
            bank = psum.tile([P, BANK], F32, name="acc_" + stream, tag=stream)
            nc.tensor.matmul_mx(
                out=bank[:],
                lhsT=x_codes[:, P * i:P * (i + 1)].bitcast(FP8X4),
                lhsT_scale=x_scales[:, P * i:P * (i + 1)],
                rhs=w_codes[:, BANK * c:BANK * (c + 1)].bitcast(FP8X4),
                rhs_scale=w_scales[:, BANK * c:BANK * (c + 1)],
                start=True,
                stop=True,
            )
            return bank

        def square_sum(bank, i, pos):
            junk = scrap.tile([P, BANK], BF16, name="junk")
            nc.scalar.activation(
                out=junk[:], in_=bank[:], func=ACT.Square,
                accum_out=sumsq[:, BANKS * i + pos:BANKS * i + pos + 1],
            )

        def norm(i):
            s = BANKS * i
            nc.gpsimd.tensor_scalar(
                out=part[:, i:i + 1], in0=sumsq[:, s:s + 1],
                scalar1=sumsq[:, s + 1:s + 2], scalar2=sumsq[:, s + 2:s + 3],
                op0=ALU.add, op1=ALU.add,
            )
            nc.gpsimd.tensor_scalar(
                out=normsq[:, i:i + 1], in0=sumsq[:, s + 3:s + 4],
                scalar1=part[:, i:i + 1], scalar2=EPS * EPS,
                op0=ALU.add, op1=ALU.max,
            )
            nc.gpsimd.tensor_tensor(
                out=roots[:, 2 * i:2 * i + 2], in0=normsq[:, i:i + 1].to_broadcast([P, 2]), in1=exponents[:], op=ALU.pow,
            )

        def exponentials(i):
            nc.scalar.activation(
                out=halves[:, 2 * i:2 * i + 2], in_=plus_minus[:], func=ACT.Exp,
                scale=roots[:, 2 * i:2 * i + 1], bias=-math.log(2.0),
                accum_out=result[:, ROW * i:ROW * i + 1],
            )

        def factor_of(i):
            return factor_v[:, i:i + 1] if i in VECTOR_FACTORS else factor[:, i:i + 1]

        def make_factor(i):
            engine = nc.vector if i in VECTOR_FACTORS else nc.gpsimd
            engine.tensor_scalar(
                out=factor_of(i), in0=halves[:, 2 * i:2 * i + 1],
                scalar1=halves[:, 2 * i + 1:2 * i + 2], scalar2=roots[:, 2 * i + 1:2 * i + 2],
                op0=ALU.subtract, op1=ALU.mult,
            )

        def scale_out(on_scalar, bank, i, c):
            lo = ROW * i + 1 + BANK * c
            dst = result[:, lo:lo + BANK]
            if on_scalar:
                nc.scalar.activation(out=dst, in_=bank[:], func=ACT.Copy, scale=factor_of(i))
            else:
                nc.vector.tensor_scalar(out=dst, in0=bank[:], scalar1=factor_of(i), scalar2=None, op0=ALU.mult)

        pieces = []
        b0 = 0
        for width in STORE_BANKS:
            b1 = b0 + width - 1
            pieces.append((b0, b1, BANK * b0, BANK * (b1 + 1) if b1 < BANKS * TILES - 1 else TILES * ROW))
            b0 += width
        scaled = set()
        exp_written = set()
        stored = set()

        def store_what_is_ready():
            for q in range(len(pieces)):
                first, last, lo, hi = pieces[q]
                if q in stored or first // BANKS not in exp_written:
                    continue
                if all(b in scaled for b in range(max(first - 1, 0), last + 1)):
                    nc.sync.dma_start(out=out_v[:, lo:hi], in_=result[:, lo:hi])
                    stored.add(q)

        squares = list(FIRST_SQUARES)
        for i in range(3, TILES):
            for c in range(BANKS):
                squares.append((i, c))
        last_square = {}
        for n in range(len(squares)):
            last_square[squares[n][0]] = n
        scalar_list = []
        for n in range(len(squares)):
            i, c = squares[n]
            scalar_list.append(("square", i, c))
            for j in range(TILES - 1):
                if n == last_square[j] + (EXP_BEHIND_FIRST if j == 0 else EXP_BEHIND):
                    scalar_list.append(("exp", j))
            if n == last_square[i]:
                scalar_list.append(("norm", i))
        for i, c in SCALAR_SCALES:
            if i == TILES - 1 and ("exp", i) not in scalar_list:
                scalar_list.append(("exp", i))
            scalar_list.append(("scale", i, c))

        vector_list = []
        for i in range(TILES):
            for c in range(BANKS):
                if (i, c) not in SCALAR_SCALES:
                    vector_list.append(("scale", i, c))

        reads_bank = ("square", "scale")
        streams = {
            "scalar": [item for item in scalar_list if item[0] in reads_bank],
            "vector": [item for item in vector_list if item[0] in reads_bank],
        }
        made = {"scalar": 0, "vector": 0}
        banks = {}
        squares_done = {}

        def next_product(stream):
            if made[stream] < len(streams[stream]):
                item = streams[stream][made[stream]]
                banks[(stream,) + item] = product(item[1], item[2], stream)
                made[stream] += 1

        def run(on_scalar, item):
            stream = "scalar" if on_scalar else "vector"
            kind = item[0]
            i = item[1]
            if kind == "square":
                square_sum(banks[(stream,) + item], i, squares_done.get(i, 0))
                squares_done[i] = squares_done.get(i, 0) + 1
                next_product(stream)
            elif kind == "norm":
                norm(i)
            elif kind == "exp":
                exponentials(i)
                exp_written.add(i)
                make_factor(i)
            elif kind == "scale":
                scale_out(on_scalar, banks[(stream,) + item], i, item[2])
                scaled.add(BANKS * i + item[2])
                next_product(stream)
                store_what_is_ready()

        ctx.enter_context(tc.manual_schedule())

        transpose_x(0)
        widen(False, 0)
        widen(True, 3)
        copy_x(True, 0)
        interleave(False, 0, BANK)
        widen(False, 1)
        widen(True, 2)
        quantize_w(0)
        quantize_x(0)
        for g in (1, 2, 3):
            transpose_x(g)
        copy_x(True, 1)
        interleave(False, BANK, 2 * BANK)
        interleave(False, 3 * BANK, 4 * BANK)
        quantize_w(1)
        quantize_x(1)
        interleave(True, 3 * BANK - SCALAR_COLUMNS, 3 * BANK)
        interleave(False, 2 * BANK, 3 * BANK - SCALAR_COLUMNS)
        quantize_w(3)
        quantize_w(2)
        copy_x(False, 2)
        copy_x(False, 3)
        quantize_x(2)
        quantize_x(3)

        for q in range(AHEAD):
            next_product("scalar")
        written = {"vector": 0}

        def advance(target):
            while written["vector"] < min(target, len(vector_list)):
                item = vector_list[written["vector"]]
                if item[1] not in exp_written:
                    return
                run(False, item)
                written["vector"] += 1

        read_by_scalar = 0
        for item in scalar_list:
            run(True, item)
            if item == ("norm", 0):
                for q in range(AHEAD):
                    next_product("vector")
            if item[0] in reads_bank:
                read_by_scalar += 1
                advance(read_by_scalar - LAG)
        advance(len(vector_list))
